import numpy as np
import ml_dtypes


def mxq(x, axis, fmt="e4m3"):
    dtype, down = {"e4m3": (ml_dtypes.float8_e4m3fn, 7), "e5m2": (ml_dtypes.float8_e5m2, 14)}[fmt]
    v = np.moveaxis(np.asarray(x, np.float32).astype(ml_dtypes.bfloat16).astype(np.float64), axis, -1)
    blocks = v.reshape(v.shape[:-1] + (-1, 32))
    amax = np.abs(blocks).max(-1, keepdims=True)
    byte = np.maximum(np.where(amax > 0, np.frexp(amax)[1] - 1 + 127, 0) - down, 1)
    scale = np.exp2(byte - 127.0)
    codes = (blocks / scale).astype(np.float32).astype(dtype).astype(np.float64)
    return np.moveaxis((codes * scale).reshape(v.shape), -1, axis)


WIDE = False


def mx_kscale(k):
    if not WIDE:
        return np.ones(k)
    levels = np.array([10, -10, 5, -5, 0])
    if k % 512:
        return np.exp2(np.random.permutation(np.resize(levels, k // 32))).repeat(32)
    a = np.empty((k // 512, 16))
    for p in range(k // 512):
        a[p, :8] = np.random.permutation(np.resize(levels, 8))
        for g in range(8):
            far = levels[np.abs(levels - a[p, g]) >= 10]
            a[p, g + 8] = far[np.random.randint(len(far))]
    return np.exp2(a.ravel()).repeat(32)


BF16 = ml_dtypes.bfloat16


def bf(x):
    return np.asarray(x, np.float32).astype(BF16)


def f64(x):
    return np.asarray(x).astype(np.float64)


B, I, H = 128, 2048, 2048
EPS = 1e-5


def sigmoid(v):
    return 1.0 / (1.0 + np.exp(-v))


def ln(v, g, b):
    m = v.mean(-1, keepdims=True)
    var = np.square(v - m).mean(-1, keepdims=True)
    return (v - m) / np.sqrt(var + EPS) * g + b


def setup_inputs():
    s, t = mx_kscale(I), mx_kscale(H)
    d = {"x": bf(np.random.standard_normal((B, I)) * s), "h": bf(np.random.standard_normal((B, H)) * t),
         "c": bf(np.random.standard_normal((B, H))), "ic_tilde": bf(0.35 * np.random.standard_normal((B, H)))}
    for g in ("f", "o"):
        d["W" + g + "_w"] = bf(np.random.standard_normal((H, I)) / np.sqrt(I) / s[None, :])
        d["W" + g + "_b"] = bf(np.random.standard_normal(H) * 0.5)
        d["U" + g + "_w"] = bf(np.random.standard_normal((H, H)) / np.sqrt(H) / t[None, :])
        d["ln" + g + "_g"] = bf(1.0 + 0.2 * np.random.standard_normal(H))
        d["ln" + g + "_b"] = bf(0.2 * np.random.standard_normal(H))
    return d


def reference(x, h, c, ic_tilde, Wf_w, Wf_b, Uf_w, lnf_g, lnf_b, Wo_w, Wo_b, Uo_w, lno_g, lno_b):
    xq = mxq(f64(x), 1, "e4m3")
    hq = mxq(f64(h), 1, "e4m3")
    pre_f = (xq @ mxq(f64(Wf_w), 1, "e4m3").T) + f64(Wf_b) + (hq @ mxq(f64(Uf_w), 1, "e4m3").T)
    pre_o = (xq @ mxq(f64(Wo_w), 1, "e4m3").T) + f64(Wo_b) + (hq @ mxq(f64(Uo_w), 1, "e4m3").T)
    f = sigmoid(ln(pre_f, f64(lnf_g), f64(lnf_b)))
    o = sigmoid(ln(pre_o, f64(lno_g), f64(lno_b)))
    c_new = f * f64(c) + f64(ic_tilde)
    h_new = o * np.tanh(c_new)
    return (h_new, c_new)

@@ -1,0 +1,293 @@
+from contextlib import ExitStack
+
+import concourse.mybir as mybir
+from concourse.masks import make_identity
+
+F32 = mybir.dt.float32
+BF16 = mybir.dt.bfloat16
+U32 = mybir.dt.uint32
+U8 = mybir.dt.uint8
+I32 = mybir.dt.int32
+FP8X4 = mybir.dt.float8_e4m3fn_x4
+ALU = mybir.AluOpType
+ACT = mybir.ActivationFunctionType
+
+P = 128
+WIDTH = 2048
+K_PASS = 512
+PASSES = WIDTH // K_PASS
+BLOCK = 256
+ROWS_EACH = BLOCK // P
+BANK = 512
+CHUNKS = WIDTH // BANK
+UNITS_PER_GATE = 2 * WIDTH // BLOCK
+UNITS = 2 * UNITS_PER_GATE
+UNITS_PER_BANK = 2 * BANK // BLOCK
+EPS = 1e-5
+
+UNITS_PER_RUN = 1
+LAG = 2
+VECTOR_SHARE = 8
+PREFETCH = 3
+
+FLOPS = 2 * P * (2 * WIDTH) * (2 * WIDTH)
+
+
+def tile_layernormlstmcell_pb_kernel(
+    tc, x, h, c, ic_tilde, Wf_w, Wf_b, Uf_w, lnf_g, lnf_b, Wo_w, Wo_b, Uo_w, lno_g, lno_b, out_0, out_1
+):
+    nc = tc.nc
+    with ExitStack() as ctx:
+        ctx.enter_context(tc.manual_schedule())
+        keep = ctx.enter_context(tc.tile_pool(name="keep", bufs=1))
+        stage = ctx.enter_context(tc.tile_pool(name="stage", bufs=2))
+        raw_pool = ctx.enter_context(tc.tile_pool(name="raw", bufs=6))
+        grouped_pool = ctx.enter_context(tc.tile_pool(name="grouped", bufs=3))
+        packed_pool = ctx.enter_context(tc.tile_pool(name="packed", bufs=LAG + UNITS_PER_RUN + 1))
+        flip_psum = ctx.enter_context(tc.psum_pool(name="flip", bufs=6))
+        sum_psum = ctx.enter_context(tc.psum_pool(name="sums", bufs=2))
+
+        ident_f32 = keep.tile([P, P], F32)
+        make_identity(nc, ident_f32[:])
+        ident_bf16 = keep.tile([P, P], BF16)
+        make_identity(nc, ident_bf16[:])
+        minus_half = keep.tile([P, 1], F32)
+        nc.vector.memset(minus_half[:], -0.5)
+
+        vectors = {"f_bias": Wf_b, "f_gain": lnf_g, "f_shift": lnf_b, "o_bias": Wo_b, "o_gain": lno_g, "o_shift": lno_b}
+        vector_names = list(vectors)
+        vector_rows = keep.tile([P, WIDTH], BF16)
+        nc.vector.memset(vector_rows[:].bitcast(I32), 0)
+
+        def load_vector(queue, r):
+            queue.dma_start(out=vector_rows[r : r + 1, :], in_=vectors[vector_names[r]].rearrange("(o n) -> o n", o=1))
+
+        for r in range(3):
+            load_vector(nc.scalar, r)
+        table_warm = keep.tile([P, 1], F32)
+        nc.scalar.activation(out=table_warm[:], in_=minus_half[:], func=ACT.Sigmoid)
+
+        spread = {}
+
+        def spread_vector(r):
+            name = vector_names[r]
+            spread[name] = keep.tile([P, WIDTH], BF16, name="spread_" + name)
+            for half in range(2):
+                copies = flip_psum.tile([P, 2 * BANK], BF16, tag="flip")
+                for q in range(2):
+                    first = (2 * half + q) * BANK
+                    nc.tensor.matmul(
+                        out=copies[:, q * BANK : (q + 1) * BANK],
+                        lhsT=ident_bf16[:, r : r + 1].to_broadcast([P, P]),
+                        rhs=vector_rows[:, first : first + BANK],
+                        start=True,
+                        stop=True,
+                    )
+                copy_out = nc.scalar.copy if half == 0 else nc.vector.tensor_copy
+                copy_out(out=spread[name][:, half * 2 * BANK : (half + 1) * 2 * BANK], in_=copies[:])
+
+        weights = {"f": (Wf_w, Uf_w), "o": (Wo_w, Uo_w)}
+        raw_of = {}
+
+        def load(i):
+            a = "f" if i < UNITS_PER_GATE else "o"
+            block, which = divmod(i % UNITS_PER_GATE, 2)
+            rows = weights[a][which][block * BLOCK : (block + 1) * BLOCK, :]
+            raw_of[i] = raw_pool.tile([P, ROWS_EACH, WIDTH], BF16, name="raw", tag="raw")
+            nc.sync.dma_start(out=raw_of[i][:], in_=rows.rearrange("(j s) k -> j s k", s=ROWS_EACH))
+
+        act_raw = {}
+        for name, source in (("x", x), ("h", h)):
+            act_raw[name] = keep.tile([P, WIDTH], BF16, name="raw_" + name)
+            nc.sync.dma_start(out=act_raw[name][:], in_=source)
+        for i in range(PREFETCH):
+            load(i)
+
+        act_codes = {}
+        act_scales = {}
+        for name in ("x", "h"):
+            act_words = act_raw[name][:].bitcast(F32)
+            act_grouped = stage.tile([P, PASSES * P * 4], BF16, align_bytes=64)
+            act_grouped_words = act_grouped[:].bitcast(F32)
+            for pair in range(PASSES // 2):
+                flipped = flip_psum.tile([P, 2, 2, P], F32, tag="flip")
+                for g in (2 * pair, 2 * pair + 1):
+                    for u in range(2):
+                        words = slice(2 * P * g + u, 2 * P * (g + 1), 2)
+                        nc.tensor.transpose(flipped[:, g % 2, u, :], act_words[:, words], ident_f32[:])
+                copy_out = nc.scalar.copy if pair == 0 else nc.vector.tensor_copy
+                copy_out(
+                    out=act_grouped_words[:, pair * BANK : (pair + 1) * BANK].rearrange("p (g b u) -> p g b u", g=2, u=2),
+                    in_=flipped[:].rearrange("p g u b -> p g b u"),
+                )
+            act_codes[name] = keep.tile([P, PASSES * P], U32, align_bytes=64, name="codes_" + name)
+            act_scales[name] = keep.tile([P, PASSES * P], U8, align_bytes=64, name="scales_" + name)
+            nc.vector.quantize_mx(out=act_codes[name][:].bitcast(FP8X4), scales=act_scales[name][:], in_=act_grouped[:])
+
+        spread_vector(0)
+        for r in range(3, 6):
+            load_vector(nc.sync, r)
+
+        pre = {}
+        normed = {}
+        gate = {}
+        stats = {}
+        mean_var = {}
+        var_eps = {}
+        rstd = {}
+        for a in ("f", "o"):
+            pre[a] = keep.tile([P, WIDTH], F32, name="pre_" + a)
+            normed[a] = keep.tile([P, WIDTH], F32, name="normed_" + a)
+            gate[a] = keep.tile([P, WIDTH], F32, name="gate_" + a)
+            stats[a] = keep.tile([P, CHUNKS, 6], F32, name="stats_" + a)
+            mean_var[a] = keep.tile([P, 2], F32, name="mean_var_" + a)
+            var_eps[a] = keep.tile([P, 1], F32, name="var_eps_" + a)
+            rstd[a] = keep.tile([P, 1], F32, name="rstd_" + a)
+        c_old = keep.tile([P, WIDTH], BF16)
+        ic_in = keep.tile([P, WIDTH], BF16)
+        c_new = keep.tile([P, WIDTH], F32)
+        tanh_c = keep.tile([P, WIDTH], F32)
+        h_new = keep.tile([P, WIDTH], F32)
+
+        def chunk_columns(chunk):
+            return slice(chunk * BANK, (chunk + 1) * BANK)
+
+        def centre_and_gain(a, cols):
+            nc.vector.scalar_tensor_tensor(
+                out=normed[a][:, cols], in0=pre[a][:, cols], scalar=mean_var[a][:, 0:1],
+                in1=spread[a + "_gain"][:, cols], op0=ALU.subtract, op1=ALU.mult,
+            )
+
+        def scale_and_shift(a, cols):
+            nc.vector.scalar_tensor_tensor(
+                out=normed[a][:, cols], in0=normed[a][:, cols], scalar=rstd[a][:, 0:1],
+                in1=spread[a + "_shift"][:, cols], op0=ALU.mult, op1=ALU.add,
+            )
+
+        def squash(a, cols):
+            nc.scalar.activation(out=gate[a][:, cols], in_=normed[a][:, cols], func=ACT.Sigmoid)
+
+        grouped_of = {}
+        codes_of = {}
+        scales_of = {}
+        sums_of = {}
+
+        def transpose_and_copy(i):
+            raw_words = raw_of[i][:].bitcast(F32)
+            grouped_of[i] = grouped_pool.tile([P, PASSES * BLOCK * 4], BF16, align_bytes=64, name="grouped", tag="grouped")
+            grouped_words = grouped_of[i][:].bitcast(F32)
+            for g in range(PASSES):
+                flipped = flip_psum.tile([P, 2, BLOCK], F32, tag="flip")
+                for u in range(2):
+                    for s in range(ROWS_EACH):
+                        words = slice(2 * P * g + u, 2 * P * (g + 1), 2)
+                        nc.tensor.transpose(flipped[:, u, s * P : (s + 1) * P], raw_words[:, s, words], ident_f32[:])
+                to_vector = (PASSES * i + g) % VECTOR_SHARE == VECTOR_SHARE - 1
+                copy_out = nc.vector.tensor_copy if to_vector else nc.scalar.copy
+                copy_out(
+                    out=grouped_words[:, g * BANK : (g + 1) * BANK].rearrange("p (n u) -> p n u", u=2),
+                    in_=flipped[:].rearrange("p u n -> p n u"),
+                )
+
+        def quantise(i):
+            codes_of[i] = packed_pool.tile([P, PASSES * BLOCK], U32, align_bytes=64, name="codes", tag="codes")
+            scales_of[i] = packed_pool.tile([P, PASSES * BLOCK], U8, align_bytes=64, name="scales", tag="scales")
+            nc.vector.quantize_mx(out=codes_of[i][:].bitcast(FP8X4), scales=scales_of[i][:], in_=grouped_of[i][:])
+
+        def multiply(i):
+            bank_number, place = divmod(i, UNITS_PER_BANK)
+            block_in_bank, which = divmod(place, 2)
+            if place == 0:
+                sums_of[bank_number] = sum_psum.tile([P, BANK], F32, name="sums", tag="sums")
+            name = "x" if which == 0 else "h"
+            for g in range(PASSES):
+                nc.tensor.matmul_mx(
+                    out=sums_of[bank_number][:, block_in_bank * BLOCK : (block_in_bank + 1) * BLOCK],
+                    lhsT=act_codes[name][:, g * P : (g + 1) * P].bitcast(FP8X4),
+                    lhsT_scale=act_scales[name][:, g * P : (g + 1) * P],
+                    rhs=codes_of[i][:, g * BLOCK : (g + 1) * BLOCK].bitcast(FP8X4),
+                    rhs_scale=scales_of[i][:, g * BLOCK : (g + 1) * BLOCK],
+                    start=(which == 0 and g == 0),
+                    stop=(which == 1 and g == PASSES - 1),
+                )
+
+        def add_bias_and_count(bank_number):
+            a = "f" if bank_number < CHUNKS else "o"
+            chunk = bank_number % CHUNKS
+            cols = chunk_columns(chunk)
+            nc.vector.tensor_tensor(
+                out=pre[a][:, cols].rearrange("p (b j s) -> p b j s", b=2, s=ROWS_EACH),
+                in0=sums_of[bank_number][:].rearrange("p (b s j) -> p b j s", b=2, s=ROWS_EACH),
+                in1=spread[a + "_bias"][:, cols].rearrange("p (b j s) -> p b j s", b=2, s=ROWS_EACH),
+                op=ALU.add,
+            )
+            nc.vector.bn_stats(out=stats[a][:, chunk, :], in_=pre[a][:, cols])
+
+        def mean_and_rstd(a):
+            nc.vector.bn_aggr(out=mean_var[a][:], in_=stats[a][:].rearrange("p n six -> p (n six)"))
+            nc.vector.tensor_scalar_add(out=var_eps[a][:], in0=mean_var[a][:, 1:2], scalar1=EPS)
+            nc.gpsimd.tensor_tensor(out=rstd[a][:], in0=var_eps[a][:], in1=minus_half[:], op=ALU.pow)
+
+        STEPS = 4 * CHUNKS
+
+        def forget_step_on_vector(step_number):
+            chunk, second = divmod(step_number % (2 * CHUNKS), 2)
+            cols = chunk_columns(chunk)
+            if step_number < 2 * CHUNKS:
+                if not second:
+                    centre_and_gain("f", cols)
+                else:
+                    scale_and_shift("f", cols)
+            else:
+                if not second:
+                    nc.vector.tensor_mul(out=c_new[:, cols], in0=gate["f"][:, cols], in1=c_old[:, cols])
+                else:
+                    nc.vector.tensor_add(out=c_new[:, cols], in0=c_new[:, cols], in1=ic_in[:, cols])
+
+        def forget_step_on_scalar(step_number):
+            chunk, second = divmod(step_number % (2 * CHUNKS), 2)
+            cols = chunk_columns(chunk)
+            if second and step_number < 2 * CHUNKS:
+                squash("f", cols)
+            if second and step_number >= 2 * CHUNKS:
+                nc.scalar.activation(out=tanh_c[:, cols], in_=c_new[:, cols], func=ACT.Tanh)
+
+        first_step_unit = UNITS_PER_GATE + LAG
+        for run_start in range(0, UNITS + LAG + 1, UNITS_PER_RUN):
+            run = range(run_start, run_start + UNITS_PER_RUN)
+            for i in run:
+                if i + PREFETCH == UNITS_PER_GATE:
+                    nc.sync.dma_start(out=c_old[:], in_=c)
+                    nc.sync.dma_start(out=ic_in[:], in_=ic_tilde)
+                if i + PREFETCH < UNITS:
+                    load(i + PREFETCH)
+                if 1 <= i <= UNITS:
+                    quantise(i - 1)
+                if 0 <= i - first_step_unit < STEPS:
+                    forget_step_on_vector(i - first_step_unit)
+                if i < UNITS:
+                    transpose_and_copy(i)
+                if 0 <= i - first_step_unit - 1 < STEPS:
+                    forget_step_on_scalar(i - first_step_unit - 1)
+            for i in run:
+                if LAG <= i < UNITS + LAG:
+                    multiply(i - LAG)
+                    if (i - LAG) % UNITS_PER_BANK == UNITS_PER_BANK - 1:
+                        add_bias_and_count((i - LAG) // UNITS_PER_BANK)
+                    if i - LAG == UNITS_PER_GATE - 1:
+                        mean_and_rstd("f")
+            if run_start // UNITS_PER_RUN + 1 < len(vector_names):
+                spread_vector(run_start // UNITS_PER_RUN + 1)
+
+        nc.sync.dma_start(out=out_1, in_=c_new[:])
+
+        mean_and_rstd("o")
+        for chunk in range(CHUNKS):
+            centre_and_gain("o", chunk_columns(chunk))
+        for chunk in range(CHUNKS):
+            scale_and_shift("o", chunk_columns(chunk))
+            squash("o", chunk_columns(chunk))
+        for chunk in range(CHUNKS):
+            cols = chunk_columns(chunk)
+            nc.vector.tensor_mul(out=h_new[:, cols], in0=gate["o"][:, cols], in1=tanh_c[:, cols])
+            nc.sync.dma_start(out=out_0[:, cols], in_=h_new[:, cols])

@@ -20,15 +20,17 @@ BLOCK = 256
 ROWS_EACH = BLOCK // P
 BANK = 512
 CHUNKS = WIDTH // BANK
+HALF = WIDTH // 2
 UNITS_PER_GATE = 2 * WIDTH // BLOCK
 UNITS = 2 * UNITS_PER_GATE
 UNITS_PER_BANK = 2 * BANK // BLOCK
 EPS = 1e-5
 
-UNITS_PER_RUN = 1
 LAG = 2
-VECTOR_SHARE = 8
 PREFETCH = 3
+SORTED_PASSES = 2
+FIRST_SORTED = PASSES - SORTED_PASSES
+PASS_WORDS = K_PASS // 2
 
 FLOPS = 2 * P * (2 * WIDTH) * (2 * WIDTH)
 
@@ -42,8 +44,9 @@ def tile_layernormlstmcell_pb_kernel(
         keep = ctx.enter_context(tc.tile_pool(name="keep", bufs=1))
         stage = ctx.enter_context(tc.tile_pool(name="stage", bufs=2))
         raw_pool = ctx.enter_context(tc.tile_pool(name="raw", bufs=6))
+        sorted_pool = ctx.enter_context(tc.tile_pool(name="sorted", bufs=3))
         grouped_pool = ctx.enter_context(tc.tile_pool(name="grouped", bufs=3))
-        packed_pool = ctx.enter_context(tc.tile_pool(name="packed", bufs=LAG + UNITS_PER_RUN + 1))
+        packed_pool = ctx.enter_context(tc.tile_pool(name="packed", bufs=LAG + 2))
         flip_psum = ctx.enter_context(tc.psum_pool(name="flip", bufs=6))
         sum_psum = ctx.enter_context(tc.psum_pool(name="sums", bufs=2))
 
@@ -62,29 +65,30 @@ def tile_layernormlstmcell_pb_kernel(
         def load_vector(queue, r):
             queue.dma_start(out=vector_rows[r : r + 1, :], in_=vectors[vector_names[r]].rearrange("(o n) -> o n", o=1))
 
-        for r in range(3):
-            load_vector(nc.scalar, r)
         table_warm = keep.tile([P, 1], F32)
         nc.scalar.activation(out=table_warm[:], in_=minus_half[:], func=ACT.Sigmoid)
 
-        spread = {}
+        in_psum = {}
 
-        def spread_vector(r):
-            name = vector_names[r]
-            spread[name] = keep.tile([P, WIDTH], BF16, name="spread_" + name)
-            for half in range(2):
-                copies = flip_psum.tile([P, 2 * BANK], BF16, tag="flip")
-                for q in range(2):
-                    first = (2 * half + q) * BANK
-                    nc.tensor.matmul(
-                        out=copies[:, q * BANK : (q + 1) * BANK],
-                        lhsT=ident_bf16[:, r : r + 1].to_broadcast([P, P]),
-                        rhs=vector_rows[:, first : first + BANK],
-                        start=True,
-                        stop=True,
-                    )
-                copy_out = nc.scalar.copy if half == 0 else nc.vector.tensor_copy
-                copy_out(out=spread[name][:, half * 2 * BANK : (half + 1) * 2 * BANK], in_=copies[:])
+        def spread_half(name, half):
+            r = vector_names.index(name)
+            in_psum[name, half] = flip_psum.tile([P, HALF], BF16, name="flip", tag="flip")
+            for q in range(HALF // BANK):
+                first = half * HALF + q * BANK
+                nc.tensor.matmul(
+                    out=in_psum[name, half][:, q * BANK : (q + 1) * BANK],
+                    lhsT=ident_bf16[:, r : r + 1].to_broadcast([P, P]),
+                    rhs=vector_rows[:, first : first + BANK],
+                    start=True,
+                    stop=True,
+                )
+
+        bias = {}
+        for a in ("f", "o"):
+            bias[a] = keep.tile([P, WIDTH], BF16, name="bias_" + a)
+
+        def keep_bias(a, half):
+            nc.vector.tensor_copy(out=bias[a][:, half * HALF : (half + 1) * HALF], in_=in_psum[a + "_bias", half][:])
 
         weights = {"f": (Wf_w, Uf_w), "o": (Wo_w, Uo_w)}
         raw_of = {}
@@ -100,11 +104,14 @@ def tile_layernormlstmcell_pb_kernel(
         for name, source in (("x", x), ("h", h)):
             act_raw[name] = keep.tile([P, WIDTH], BF16, name="raw_" + name)
             nc.sync.dma_start(out=act_raw[name][:], in_=source)
+        for r in range(len(vector_names)):
+            load_vector(nc.sync, r)
         for i in range(PREFETCH):
             load(i)
 
         act_codes = {}
         act_scales = {}
+        act_grouped_of = {}
         for name in ("x", "h"):
             act_words = act_raw[name][:].bitcast(F32)
             act_grouped = stage.tile([P, PASSES * P * 4], BF16, align_bytes=64)
@@ -122,16 +129,19 @@ def tile_layernormlstmcell_pb_kernel(
                 )
             act_codes[name] = keep.tile([P, PASSES * P], U32, align_bytes=64, name="codes_" + name)
             act_scales[name] = keep.tile([P, PASSES * P], U8, align_bytes=64, name="scales_" + name)
-            nc.vector.quantize_mx(out=act_codes[name][:].bitcast(FP8X4), scales=act_scales[name][:], in_=act_grouped[:])
+            act_grouped_of[name] = act_grouped
 
-        spread_vector(0)
-        for r in range(3, 6):
-            load_vector(nc.sync, r)
+        def quantise_activation(name):
+            nc.vector.quantize_mx(
+                out=act_codes[name][:].bitcast(FP8X4), scales=act_scales[name][:], in_=act_grouped_of[name][:]
+            )
+
 
         pre = {}
         normed = {}
         gate = {}
         stats = {}
+        stats_slots = {"f": 0, "o": 0}
         mean_var = {}
         var_eps = {}
         rstd = {}
@@ -139,7 +149,7 @@ def tile_layernormlstmcell_pb_kernel(
             pre[a] = keep.tile([P, WIDTH], F32, name="pre_" + a)
             normed[a] = keep.tile([P, WIDTH], F32, name="normed_" + a)
             gate[a] = keep.tile([P, WIDTH], F32, name="gate_" + a)
-            stats[a] = keep.tile([P, CHUNKS, 6], F32, name="stats_" + a)
+            stats[a] = keep.tile([P, CHUNKS + 1, 6], F32, name="stats_" + a)
             mean_var[a] = keep.tile([P, 2], F32, name="mean_var_" + a)
             var_eps[a] = keep.tile([P, 1], F32, name="var_eps_" + a)
             rstd[a] = keep.tile([P, 1], F32, name="rstd_" + a)
@@ -152,25 +162,42 @@ def tile_layernormlstmcell_pb_kernel(
         def chunk_columns(chunk):
             return slice(chunk * BANK, (chunk + 1) * BANK)
 
+        def half_columns(half):
+            return slice(half * HALF, (half + 1) * HALF)
+
+        def spread_columns(name, cols):
+            first = cols.start % HALF
+            return in_psum[name, cols.start // HALF][:, first : first + cols.stop - cols.start]
+
         def centre_and_gain(a, cols):
             nc.vector.scalar_tensor_tensor(
                 out=normed[a][:, cols], in0=pre[a][:, cols], scalar=mean_var[a][:, 0:1],
-                in1=spread[a + "_gain"][:, cols], op0=ALU.subtract, op1=ALU.mult,
+                in1=spread_columns(a + "_gain", cols), op0=ALU.subtract, op1=ALU.mult,
             )
 
         def scale_and_shift(a, cols):
             nc.vector.scalar_tensor_tensor(
                 out=normed[a][:, cols], in0=normed[a][:, cols], scalar=rstd[a][:, 0:1],
-                in1=spread[a + "_shift"][:, cols], op0=ALU.mult, op1=ALU.add,
+                in1=spread_columns(a + "_shift", cols), op0=ALU.mult, op1=ALU.add,
             )
 
         def squash(a, cols):
             nc.scalar.activation(out=gate[a][:, cols], in_=normed[a][:, cols], func=ACT.Sigmoid)
 
+        sorted_of = {}
         grouped_of = {}
         codes_of = {}
         scales_of = {}
         sums_of = {}
+
+        def sort_words(i):
+            sorted_of[i] = sorted_pool.tile([P, ROWS_EACH, SORTED_PASSES, 2, P], F32, name="sorted", tag="sorted")
+            nc.vector.tensor_copy(
+                out=sorted_of[i][:],
+                in_=raw_of[i][:].bitcast(F32)[:, :, FIRST_SORTED * PASS_WORDS :].rearrange(
+                    "p s (g x u) -> p s g u x", g=SORTED_PASSES, u=2
+                ),
+            )
 
         def transpose_and_copy(i):
             raw_words = raw_of[i][:].bitcast(F32)
@@ -180,19 +207,27 @@ def tile_layernormlstmcell_pb_kernel(
                 flipped = flip_psum.tile([P, 2, BLOCK], F32, tag="flip")
                 for u in range(2):
                     for s in range(ROWS_EACH):
-                        words = slice(2 * P * g + u, 2 * P * (g + 1), 2)
-                        nc.tensor.transpose(flipped[:, u, s * P : (s + 1) * P], raw_words[:, s, words], ident_f32[:])
-                to_vector = (PASSES * i + g) % VECTOR_SHARE == VECTOR_SHARE - 1
-                copy_out = nc.vector.tensor_copy if to_vector else nc.scalar.copy
-                copy_out(
+                        if g < FIRST_SORTED:
+                            words = raw_words[:, s, PASS_WORDS * g + u : PASS_WORDS * (g + 1) : 2]
+                        else:
+                            words = sorted_of[i][:, s, g - FIRST_SORTED, u, :]
+                        nc.tensor.transpose(flipped[:, u, s * P : (s + 1) * P], words, ident_f32[:])
+                nc.scalar.copy(
                     out=grouped_words[:, g * BANK : (g + 1) * BANK].rearrange("p (n u) -> p n u", u=2),
                     in_=flipped[:].rearrange("p u n -> p n u"),
                 )
 
-        def quantise(i):
+        def quantise(i, parts=1):
             codes_of[i] = packed_pool.tile([P, PASSES * BLOCK], U32, align_bytes=64, name="codes", tag="codes")
             scales_of[i] = packed_pool.tile([P, PASSES * BLOCK], U8, align_bytes=64, name="scales", tag="scales")
-            nc.vector.quantize_mx(out=codes_of[i][:].bitcast(FP8X4), scales=scales_of[i][:], in_=grouped_of[i][:])
+            width = PASSES * BLOCK // parts
+            for part in range(parts):
+                cols = slice(part * width, (part + 1) * width)
+                nc.vector.quantize_mx(
+                    out=codes_of[i][:, cols].bitcast(FP8X4),
+                    scales=scales_of[i][:, cols],
+                    in_=grouped_of[i][:, 4 * cols.start : 4 * cols.stop],
+                )
 
         def multiply(i):
             bank_number, place = divmod(i, UNITS_PER_BANK)
@@ -211,83 +246,106 @@ def tile_layernormlstmcell_pb_kernel(
                     stop=(which == 1 and g == PASSES - 1),
                 )
 
-        def add_bias_and_count(bank_number):
+        def add_bias_and_count(bank_number, first_block, blocks):
             a = "f" if bank_number < CHUNKS else "o"
             chunk = bank_number % CHUNKS
-            cols = chunk_columns(chunk)
+            first = chunk * BANK + first_block * BLOCK
+            cols = slice(first, first + blocks * BLOCK)
+            sums = sums_of[bank_number][:, first_block * BLOCK : (first_block + blocks) * BLOCK]
+            slot = stats_slots[a]
+            stats_slots[a] += 1
             nc.vector.tensor_tensor(
-                out=pre[a][:, cols].rearrange("p (b j s) -> p b j s", b=2, s=ROWS_EACH),
-                in0=sums_of[bank_number][:].rearrange("p (b s j) -> p b j s", b=2, s=ROWS_EACH),
-                in1=spread[a + "_bias"][:, cols].rearrange("p (b j s) -> p b j s", b=2, s=ROWS_EACH),
+                out=pre[a][:, cols].rearrange("p (b j s) -> p b j s", b=blocks, s=ROWS_EACH),
+                in0=sums.rearrange("p (b s j) -> p b j s", b=blocks, s=ROWS_EACH),
+                in1=bias[a][:, cols].rearrange("p (b j s) -> p b j s", b=blocks, s=ROWS_EACH),
                 op=ALU.add,
             )
-            nc.vector.bn_stats(out=stats[a][:, chunk, :], in_=pre[a][:, cols])
+            nc.vector.bn_stats(out=stats[a][:, slot, :], in_=pre[a][:, cols])
 
         def mean_and_rstd(a):
-            nc.vector.bn_aggr(out=mean_var[a][:], in_=stats[a][:].rearrange("p n six -> p (n six)"))
+            nc.vector.bn_aggr(out=mean_var[a][:], in_=stats[a][:, : stats_slots[a], :].rearrange("p n six -> p (n six)"))
             nc.vector.tensor_scalar_add(out=var_eps[a][:], in0=mean_var[a][:, 1:2], scalar1=EPS)
             nc.gpsimd.tensor_tensor(out=rstd[a][:], in0=var_eps[a][:], in1=minus_half[:], op=ALU.pow)
 
-        STEPS = 4 * CHUNKS
+        STEPS = ("gain", 0), ("gain", 1), ("shift", 0), ("shift", 1), ("mul", 0), ("mul", 1), ("add", 0), ("add", 1)
 
-        def forget_step_on_vector(step_number):
-            chunk, second = divmod(step_number % (2 * CHUNKS), 2)
-            cols = chunk_columns(chunk)
-            if step_number < 2 * CHUNKS:
-                if not second:
-                    centre_and_gain("f", cols)
-                else:
-                    scale_and_shift("f", cols)
+        def forget_step_on_vector(kind, half):
+            cols = half_columns(half)
+            if kind == "gain":
+                centre_and_gain("f", cols)
+            elif kind == "shift":
+                scale_and_shift("f", cols)
+            elif kind == "mul":
+                nc.vector.tensor_mul(out=c_new[:, cols], in0=gate["f"][:, cols], in1=c_old[:, cols])
             else:
-                if not second:
-                    nc.vector.tensor_mul(out=c_new[:, cols], in0=gate["f"][:, cols], in1=c_old[:, cols])
-                else:
-                    nc.vector.tensor_add(out=c_new[:, cols], in0=c_new[:, cols], in1=ic_in[:, cols])
+                nc.vector.tensor_add(out=c_new[:, cols], in0=c_new[:, cols], in1=ic_in[:, cols])
 
-        def forget_step_on_scalar(step_number):
-            chunk, second = divmod(step_number % (2 * CHUNKS), 2)
-            cols = chunk_columns(chunk)
-            if second and step_number < 2 * CHUNKS:
+        def forget_step_on_scalar(kind, half):
+            cols = half_columns(half)
+            if kind == "shift":
                 squash("f", cols)
-            if second and step_number >= 2 * CHUNKS:
+            elif kind == "add":
                 nc.scalar.activation(out=tanh_c[:, cols], in_=c_new[:, cols], func=ACT.Tanh)
 
         first_step_unit = UNITS_PER_GATE + LAG
-        for run_start in range(0, UNITS + LAG + 1, UNITS_PER_RUN):
-            run = range(run_start, run_start + UNITS_PER_RUN)
-            for i in run:
-                if i + PREFETCH == UNITS_PER_GATE:
-                    nc.sync.dma_start(out=c_old[:], in_=c)
-                    nc.sync.dma_start(out=ic_in[:], in_=ic_tilde)
-                if i + PREFETCH < UNITS:
-                    load(i + PREFETCH)
-                if 1 <= i <= UNITS:
-                    quantise(i - 1)
-                if 0 <= i - first_step_unit < STEPS:
-                    forget_step_on_vector(i - first_step_unit)
-                if i < UNITS:
-                    transpose_and_copy(i)
-                if 0 <= i - first_step_unit - 1 < STEPS:
-                    forget_step_on_scalar(i - first_step_unit - 1)
-            for i in run:
-                if LAG <= i < UNITS + LAG:
-                    multiply(i - LAG)
-                    if (i - LAG) % UNITS_PER_BANK == UNITS_PER_BANK - 1:
-                        add_bias_and_count((i - LAG) // UNITS_PER_BANK)
-                    if i - LAG == UNITS_PER_GATE - 1:
-                        mean_and_rstd("f")
-            if run_start // UNITS_PER_RUN + 1 < len(vector_names):
-                spread_vector(run_start // UNITS_PER_RUN + 1)
+        step_at = {}
+        for k, step in enumerate(STEPS):
+            step_at[first_step_unit + k * (UNITS - first_step_unit) // len(STEPS)] = step
+        bias_behind = {2: ("f", 0), 3: ("f", 1), 9: ("o", 0), 10: ("o", 1)}
+
+        sort_words(0)
+        for i in range(UNITS + LAG):
+            if i + PREFETCH == UNITS_PER_GATE:
+                nc.sync.dma_start(out=c_old[:], in_=c)
+                nc.sync.dma_start(out=ic_in[:], in_=ic_tilde)
+            if i + PREFETCH < UNITS:
+                load(i + PREFETCH)
+            if i + 1 < UNITS:
+                sort_words(i + 1)
+            if i == 0:
+                quantise_activation("x")
+                quantise_activation("h")
+            if 1 <= i <= UNITS:
+                quantise(i - 1, parts=2 if i == UNITS else 1)
+            if i - 1 in bias_behind:
+                keep_bias(*bias_behind[i - 1])
+            if i in step_at:
+                forget_step_on_vector(*step_at[i])
+            if i < UNITS:
+                transpose_and_copy(i)
+            if i - 1 in step_at:
+                forget_step_on_scalar(*step_at[i - 1])
+            if i >= UNITS:
+                for half in range(2):
+                    spread_half("o_gain" if i == UNITS else "o_shift", half)
+            if i >= LAG:
+                multiply(i - LAG)
+                bank_number, place = divmod(i - LAG, UNITS_PER_BANK)
+                if bank_number < 2 * CHUNKS - 1:
+                    if place == UNITS_PER_BANK - 1:
+                        add_bias_and_count(bank_number, 0, 2)
+                elif place % 2 == 1:
+                    add_bias_and_count(bank_number, place // 2, 1)
+                if i - LAG == UNITS_PER_GATE - 1:
+                    mean_and_rstd("f")
+            if i in bias_behind:
+                a, half = bias_behind[i]
+                spread_half(a + "_bias", half)
+            if i + 1 in step_at and step_at[i + 1][0] in ("gain", "shift"):
+                kind, half = step_at[i + 1]
+                spread_half("f_" + kind, half)
 
         nc.sync.dma_start(out=out_1, in_=c_new[:])
 
         mean_and_rstd("o")
-        for chunk in range(CHUNKS):
-            centre_and_gain("o", chunk_columns(chunk))
-        for chunk in range(CHUNKS):
-            scale_and_shift("o", chunk_columns(chunk))
-            squash("o", chunk_columns(chunk))
-        for chunk in range(CHUNKS):
-            cols = chunk_columns(chunk)
-            nc.vector.tensor_mul(out=h_new[:, cols], in0=gate["o"][:, cols], in1=tanh_c[:, cols])
-            nc.sync.dma_start(out=out_0[:, cols], in_=h_new[:, cols])
+        for chunks in ((0, 1), (2, 3)):
+            for chunk in chunks:
+                centre_and_gain("o", chunk_columns(chunk))
+            for chunk in chunks:
+                scale_and_shift("o", chunk_columns(chunk))
+                squash("o", chunk_columns(chunk))
+            multiplier = nc.gpsimd if 0 in chunks else nc.vector
+            for chunk in chunks:
+                cols = chunk_columns(chunk)
+                multiplier.tensor_tensor(out=h_new[:, cols], in0=gate["o"][:, cols], in1=tanh_c[:, cols], op=ALU.mult)
+                nc.sync.dma_start(out=out_0[:, cols], in_=h_new[:, cols])

@@ -28,8 +28,7 @@ EPS = 1e-5
 
 LAG = 2
 PREFETCH = 3
-SORTED_PASSES = 2
-FIRST_SORTED = PASSES - SORTED_PASSES
+VECTOR_SHARE = 16
 PASS_WORDS = K_PASS // 2
 
 FLOPS = 2 * P * (2 * WIDTH) * (2 * WIDTH)
@@ -104,9 +103,11 @@ def tile_layernormlstmcell_pb_kernel(
         for name, source in (("x", x), ("h", h)):
             act_raw[name] = keep.tile([P, WIDTH], BF16, name="raw_" + name)
             nc.sync.dma_start(out=act_raw[name][:], in_=source)
+        load(0)
+        load(1)
         for r in range(len(vector_names)):
             load_vector(nc.sync, r)
-        for i in range(PREFETCH):
+        for i in range(2, PREFETCH):
             load(i)
 
         act_codes = {}
@@ -190,29 +191,40 @@ def tile_layernormlstmcell_pb_kernel(
         scales_of = {}
         sums_of = {}
 
+        def passes_to_sort(i):
+            if i >= UNITS - 3:
+                return 0
+            return 2 if i < UNITS_PER_GATE else 1
+
         def sort_words(i):
-            sorted_of[i] = sorted_pool.tile([P, ROWS_EACH, SORTED_PASSES, 2, P], F32, name="sorted", tag="sorted")
+            passes = passes_to_sort(i)
+            if passes == 0:
+                return
+            sorted_of[i] = sorted_pool.tile([P, ROWS_EACH, passes, 2, P], F32, name="sorted", tag="sorted")
             nc.vector.tensor_copy(
                 out=sorted_of[i][:],
-                in_=raw_of[i][:].bitcast(F32)[:, :, FIRST_SORTED * PASS_WORDS :].rearrange(
-                    "p s (g x u) -> p s g u x", g=SORTED_PASSES, u=2
+                in_=raw_of[i][:].bitcast(F32)[:, :, (PASSES - passes) * PASS_WORDS :].rearrange(
+                    "p s (g x u) -> p s g u x", g=passes, u=2
                 ),
             )
 
         def transpose_and_copy(i):
             raw_words = raw_of[i][:].bitcast(F32)
+            first_sorted = PASSES - passes_to_sort(i)
             grouped_of[i] = grouped_pool.tile([P, PASSES * BLOCK * 4], BF16, align_bytes=64, name="grouped", tag="grouped")
             grouped_words = grouped_of[i][:].bitcast(F32)
             for g in range(PASSES):
                 flipped = flip_psum.tile([P, 2, BLOCK], F32, tag="flip")
                 for u in range(2):
                     for s in range(ROWS_EACH):
-                        if g < FIRST_SORTED:
+                        if g < first_sorted:
                             words = raw_words[:, s, PASS_WORDS * g + u : PASS_WORDS * (g + 1) : 2]
                         else:
-                            words = sorted_of[i][:, s, g - FIRST_SORTED, u, :]
+                            words = sorted_of[i][:, s, g - first_sorted, u, :]
                         nc.tensor.transpose(flipped[:, u, s * P : (s + 1) * P], words, ident_f32[:])
-                nc.scalar.copy(
+                to_vector = (PASSES * i + g) % VECTOR_SHARE == 1
+                copy_out = nc.vector.tensor_copy if to_vector else nc.scalar.copy
+                copy_out(
                     out=grouped_words[:, g * BANK : (g + 1) * BANK].rearrange("p (n u) -> p n u", u=2),
                     in_=flipped[:].rearrange("p u n -> p n u"),
                 )

@@ -60,6 +60,8 @@ def tile_layernormlstmcell_pb_kernel(
         vector_names = list(vectors)
         vector_rows = keep.tile([P, WIDTH], BF16)
         nc.vector.memset(vector_rows[:].bitcast(I32), 0)
+        first_row = keep.tile([P, WIDTH], BF16)
+        nc.vector.memset(first_row[:].bitcast(I32), 0)
 
         def load_vector(queue, r):
             queue.dma_start(out=vector_rows[r : r + 1, :], in_=vectors[vector_names[r]].rearrange("(o n) -> o n", o=1))
@@ -70,14 +72,15 @@ def tile_layernormlstmcell_pb_kernel(
         in_psum = {}
 
         def spread_half(name, half):
-            r = vector_names.index(name)
+            r = 0 if name == "f_bias" else vector_names.index(name)
+            rows = first_row if name == "f_bias" else vector_rows
             in_psum[name, half] = flip_psum.tile([P, HALF], BF16, name="flip", tag="flip")
             for q in range(HALF // BANK):
                 first = half * HALF + q * BANK
                 nc.tensor.matmul(
                     out=in_psum[name, half][:, q * BANK : (q + 1) * BANK],
                     lhsT=ident_bf16[:, r : r + 1].to_broadcast([P, P]),
-                    rhs=vector_rows[:, first : first + BANK],
+                    rhs=rows[:, first : first + BANK],
                     start=True,
                     stop=True,
                 )
@@ -87,7 +90,7 @@ def tile_layernormlstmcell_pb_kernel(
             bias[a] = keep.tile([P, WIDTH], BF16, name="bias_" + a)
 
         def keep_bias(a, half):
-            nc.vector.tensor_copy(out=bias[a][:, half * HALF : (half + 1) * HALF], in_=in_psum[a + "_bias", half][:])
+            nc.scalar.copy(out=bias[a][:, half * HALF : (half + 1) * HALF], in_=in_psum[a + "_bias", half][:])
 
         weights = {"f": (Wf_w, Uf_w), "o": (Wo_w, Uo_w)}
         raw_of = {}
@@ -103,9 +106,11 @@ def tile_layernormlstmcell_pb_kernel(
         for name, source in (("x", x), ("h", h)):
             act_raw[name] = keep.tile([P, WIDTH], BF16, name="raw_" + name)
             nc.sync.dma_start(out=act_raw[name][:], in_=source)
+            if name == "x":
+                nc.sync.dma_start(out=first_row[0:1, :], in_=Wf_b.rearrange("(o n) -> o n", o=1))
         load(0)
         load(1)
-        for r in range(len(vector_names)):
+        for r in range(1, len(vector_names)):
             load_vector(nc.sync, r)
         for i in range(2, PREFETCH):
             load(i)
@@ -131,6 +136,9 @@ def tile_layernormlstmcell_pb_kernel(
             act_codes[name] = keep.tile([P, PASSES * P], U32, align_bytes=64, name="codes_" + name)
             act_scales[name] = keep.tile([P, PASSES * P], U8, align_bytes=64, name="scales_" + name)
             act_grouped_of[name] = act_grouped
+        for half in range(2):
+            spread_half("f_bias", half)
+            keep_bias("f", half)
 
         def quantise_activation(name):
             nc.vector.quantize_mx(
@@ -139,7 +147,6 @@ def tile_layernormlstmcell_pb_kernel(
 
 
         pre = {}
-        normed = {}
         gate = {}
         stats = {}
         stats_slots = {"f": 0, "o": 0}
@@ -148,7 +155,6 @@ def tile_layernormlstmcell_pb_kernel(
         rstd = {}
         for a in ("f", "o"):
             pre[a] = keep.tile([P, WIDTH], F32, name="pre_" + a)
-            normed[a] = keep.tile([P, WIDTH], F32, name="normed_" + a)
             gate[a] = keep.tile([P, WIDTH], F32, name="gate_" + a)
             stats[a] = keep.tile([P, CHUNKS + 1, 6], F32, name="stats_" + a)
             mean_var[a] = keep.tile([P, 2], F32, name="mean_var_" + a)
@@ -172,18 +178,18 @@ def tile_layernormlstmcell_pb_kernel(
 
         def centre_and_gain(a, cols):
             nc.vector.scalar_tensor_tensor(
-                out=normed[a][:, cols], in0=pre[a][:, cols], scalar=mean_var[a][:, 0:1],
+                out=pre[a][:, cols], in0=pre[a][:, cols], scalar=mean_var[a][:, 0:1],
                 in1=spread_columns(a + "_gain", cols), op0=ALU.subtract, op1=ALU.mult,
             )
 
         def scale_and_shift(a, cols):
             nc.vector.scalar_tensor_tensor(
-                out=normed[a][:, cols], in0=normed[a][:, cols], scalar=rstd[a][:, 0:1],
+                out=pre[a][:, cols], in0=pre[a][:, cols], scalar=rstd[a][:, 0:1],
                 in1=spread_columns(a + "_shift", cols), op0=ALU.mult, op1=ALU.add,
             )
 
         def squash(a, cols):
-            nc.scalar.activation(out=gate[a][:, cols], in_=normed[a][:, cols], func=ACT.Sigmoid)
+            nc.scalar.activation(out=gate[a][:, cols], in_=pre[a][:, cols], func=ACT.Sigmoid)
 
         sorted_of = {}
         grouped_of = {}
@@ -191,38 +197,51 @@ def tile_layernormlstmcell_pb_kernel(
         scales_of = {}
         sums_of = {}
 
-        def passes_to_sort(i):
+        def passes_for_vector(i):
             if i >= UNITS - 3:
                 return 0
             return 2 if i < UNITS_PER_GATE else 1
 
-        def sort_words(i):
-            passes = passes_to_sort(i)
+        def passes_for_scalar(i):
+            return i%2
+
+        def sort_words(i, engine_copy, first, passes, who):
             if passes == 0:
                 return
-            sorted_of[i] = sorted_pool.tile([P, ROWS_EACH, passes, 2, P], F32, name="sorted", tag="sorted")
-            nc.vector.tensor_copy(
-                out=sorted_of[i][:],
-                in_=raw_of[i][:].bitcast(F32)[:, :, (PASSES - passes) * PASS_WORDS :].rearrange(
+            tile = sorted_pool.tile([P, ROWS_EACH, passes, 2, P], F32, name="sorted_" + who, tag="sorted_" + who)
+            engine_copy(
+                out=tile[:],
+                in_=raw_of[i][:].bitcast(F32)[:, :, first * PASS_WORDS : (first + passes) * PASS_WORDS].rearrange(
                     "p s (g x u) -> p s g u x", g=passes, u=2
                 ),
             )
+            for g in range(passes):
+                sorted_of[i, first + g] = tile, g
+
+        def sort_on_vector(i):
+            passes = passes_for_vector(i)
+            sort_words(i, nc.vector.tensor_copy, PASSES - passes_for_scalar(i) - passes, passes, "v")
+
+        def sort_on_scalar(i):
+            sort_words(i, nc.scalar.copy, PASSES - passes_for_scalar(i), passes_for_scalar(i), "s")
 
         def transpose_and_copy(i):
             raw_words = raw_of[i][:].bitcast(F32)
-            first_sorted = PASSES - passes_to_sort(i)
             grouped_of[i] = grouped_pool.tile([P, PASSES * BLOCK * 4], BF16, align_bytes=64, name="grouped", tag="grouped")
             grouped_words = grouped_of[i][:].bitcast(F32)
             for g in range(PASSES):
                 flipped = flip_psum.tile([P, 2, BLOCK], F32, tag="flip")
                 for u in range(2):
                     for s in range(ROWS_EACH):
-                        if g < first_sorted:
-                            words = raw_words[:, s, PASS_WORDS * g + u : PASS_WORDS * (g + 1) : 2]
+                        if (i, g) in sorted_of:
+                            tile, place = sorted_of[i, g]
+                            words = tile[:, s, place, u, :]
                         else:
-                            words = sorted_of[i][:, s, g - first_sorted, u, :]
+                            words = raw_words[:, s, PASS_WORDS * g + u : PASS_WORDS * (g + 1) : 2]
                         nc.tensor.transpose(flipped[:, u, s * P : (s + 1) * P], words, ident_f32[:])
-                to_vector = (PASSES * i + g) % VECTOR_SHARE == 1
+                if g == 2 and i + 1 < UNITS:
+                    sort_on_scalar(i + 1)
+                to_vector = i >= 3 and (PASSES * i + g) % VECTOR_SHARE == 1
                 copy_out = nc.vector.tensor_copy if to_vector else nc.scalar.copy
                 copy_out(
                     out=grouped_words[:, g * BANK : (g + 1) * BANK].rearrange("p (n u) -> p n u", u=2),
@@ -299,30 +318,28 @@ def tile_layernormlstmcell_pb_kernel(
             elif kind == "add":
                 nc.scalar.activation(out=tanh_c[:, cols], in_=c_new[:, cols], func=ACT.Tanh)
 
-        first_step_unit = UNITS_PER_GATE + LAG
+        first_step_unit = UNITS_PER_GATE + LAG + 1
         step_at = {}
         for k, step in enumerate(STEPS):
             step_at[first_step_unit + k * (UNITS - first_step_unit) // len(STEPS)] = step
-        bias_behind = {2: ("f", 0), 3: ("f", 1), 9: ("o", 0), 10: ("o", 1)}
+        bias_behind = {9: ("o", 0), 10: ("o", 1)}
 
-        sort_words(0)
+        sort_on_vector(0)
         for i in range(UNITS + LAG):
             if i + PREFETCH == UNITS_PER_GATE:
                 nc.sync.dma_start(out=c_old[:], in_=c)
                 nc.sync.dma_start(out=ic_in[:], in_=ic_tilde)
             if i + PREFETCH < UNITS:
                 load(i + PREFETCH)
+            if i in step_at:
+                forget_step_on_vector(*step_at[i])
             if i + 1 < UNITS:
-                sort_words(i + 1)
+                sort_on_vector(i + 1)
             if i == 0:
                 quantise_activation("x")
                 quantise_activation("h")
             if 1 <= i <= UNITS:
                 quantise(i - 1, parts=2 if i == UNITS else 1)
-            if i - 1 in bias_behind:
-                keep_bias(*bias_behind[i - 1])
-            if i in step_at:
-                forget_step_on_vector(*step_at[i])
             if i < UNITS:
                 transpose_and_copy(i)
             if i - 1 in step_at:
@@ -343,6 +360,7 @@ def tile_layernormlstmcell_pb_kernel(
             if i in bias_behind:
                 a, half = bias_behind[i]
                 spread_half(a + "_bias", half)
+                keep_bias(a, half)
             if i + 1 in step_at and step_at[i + 1][0] in ("gain", "shift"):
                 kind, half = step_at[i + 1]
                 spread_half("f_" + kind, half)

@@ -28,7 +28,8 @@ EPS = 1e-5
 
 LAG = 2
 PREFETCH = 3
-VECTOR_SHARE = 16
+BIASES = 2
+VECTOR_SHARE = 32
 PASS_WORDS = K_PASS // 2
 
 FLOPS = 2 * P * (2 * WIDTH) * (2 * WIDTH)
@@ -56,15 +57,16 @@ def tile_layernormlstmcell_pb_kernel(
         minus_half = keep.tile([P, 1], F32)
         nc.vector.memset(minus_half[:], -0.5)
 
-        vectors = {"f_bias": Wf_b, "f_gain": lnf_g, "f_shift": lnf_b, "o_bias": Wo_b, "o_gain": lno_g, "o_shift": lno_b}
+        vectors = {"f_bias": Wf_b, "o_bias": Wo_b, "f_gain": lnf_g, "f_shift": lnf_b, "o_gain": lno_g, "o_shift": lno_b}
         vector_names = list(vectors)
         vector_rows = keep.tile([P, WIDTH], BF16)
         nc.vector.memset(vector_rows[:].bitcast(I32), 0)
-        first_row = keep.tile([P, WIDTH], BF16)
-        nc.vector.memset(first_row[:].bitcast(I32), 0)
+        bias_rows = keep.tile([P, WIDTH], BF16)
+        nc.vector.memset(bias_rows[:].bitcast(I32), 0)
 
-        def load_vector(queue, r):
-            queue.dma_start(out=vector_rows[r : r + 1, :], in_=vectors[vector_names[r]].rearrange("(o n) -> o n", o=1))
+        def load_vector(r):
+            rows = bias_rows if r < BIASES else vector_rows
+            nc.sync.dma_start(out=rows[r : r + 1, :], in_=vectors[vector_names[r]].rearrange("(o n) -> o n", o=1))
 
         table_warm = keep.tile([P, 1], F32)
         nc.scalar.activation(out=table_warm[:], in_=minus_half[:], func=ACT.Sigmoid)
@@ -72,8 +74,8 @@ def tile_layernormlstmcell_pb_kernel(
         in_psum = {}
 
         def spread_half(name, half):
-            r = 0 if name == "f_bias" else vector_names.index(name)
-            rows = first_row if name == "f_bias" else vector_rows
+            r = vector_names.index(name)
+            rows = bias_rows if r < BIASES else vector_rows
             in_psum[name, half] = flip_psum.tile([P, HALF], BF16, name="flip", tag="flip")
             for q in range(HALF // BANK):
                 first = half * HALF + q * BANK
@@ -103,22 +105,25 @@ def tile_layernormlstmcell_pb_kernel(
             nc.sync.dma_start(out=raw_of[i][:], in_=rows.rearrange("(j s) k -> j s k", s=ROWS_EACH))
 
         act_raw = {}
-        for name, source in (("x", x), ("h", h)):
+
+        def load_activation(name, source):
             act_raw[name] = keep.tile([P, WIDTH], BF16, name="raw_" + name)
             nc.sync.dma_start(out=act_raw[name][:], in_=source)
-            if name == "x":
-                nc.sync.dma_start(out=first_row[0:1, :], in_=Wf_b.rearrange("(o n) -> o n", o=1))
+
+        load_activation("x", x)
+        for r in range(BIASES):
+            load_vector(r)
         load(0)
         load(1)
-        for r in range(1, len(vector_names)):
-            load_vector(nc.sync, r)
+        load_activation("h", h)
         for i in range(2, PREFETCH):
             load(i)
 
         act_codes = {}
         act_scales = {}
         act_grouped_of = {}
-        for name in ("x", "h"):
+
+        def flip_activation(name):
             act_words = act_raw[name][:].bitcast(F32)
             act_grouped = stage.tile([P, PASSES * P * 4], BF16, align_bytes=64)
             act_grouped_words = act_grouped[:].bitcast(F32)
@@ -136,6 +141,7 @@ def tile_layernormlstmcell_pb_kernel(
             act_codes[name] = keep.tile([P, PASSES * P], U32, align_bytes=64, name="codes_" + name)
             act_scales[name] = keep.tile([P, PASSES * P], U8, align_bytes=64, name="scales_" + name)
             act_grouped_of[name] = act_grouped
+        flip_activation("x")
         for half in range(2):
             spread_half("f_bias", half)
             keep_bias("f", half)
@@ -197,50 +203,37 @@ def tile_layernormlstmcell_pb_kernel(
         scales_of = {}
         sums_of = {}
 
-        def passes_for_vector(i):
-            if i >= UNITS - 3:
+        def passes_to_sort(i):
+            if i >= UNITS - 3 or i == 2:
                 return 0
             return 2 if i < UNITS_PER_GATE else 1
 
-        def passes_for_scalar(i):
-            return i%2
-
-        def sort_words(i, engine_copy, first, passes, who):
+        def sort_words(i):
+            passes = passes_to_sort(i)
             if passes == 0:
                 return
-            tile = sorted_pool.tile([P, ROWS_EACH, passes, 2, P], F32, name="sorted_" + who, tag="sorted_" + who)
-            engine_copy(
-                out=tile[:],
-                in_=raw_of[i][:].bitcast(F32)[:, :, first * PASS_WORDS : (first + passes) * PASS_WORDS].rearrange(
+            sorted_of[i] = sorted_pool.tile([P, ROWS_EACH, passes, 2, P], F32, name="sorted", tag="sorted")
+            nc.vector.tensor_copy(
+                out=sorted_of[i][:],
+                in_=raw_of[i][:].bitcast(F32)[:, :, (PASSES - passes) * PASS_WORDS :].rearrange(
                     "p s (g x u) -> p s g u x", g=passes, u=2
                 ),
             )
-            for g in range(passes):
-                sorted_of[i, first + g] = tile, g
-
-        def sort_on_vector(i):
-            passes = passes_for_vector(i)
-            sort_words(i, nc.vector.tensor_copy, PASSES - passes_for_scalar(i) - passes, passes, "v")
-
-        def sort_on_scalar(i):
-            sort_words(i, nc.scalar.copy, PASSES - passes_for_scalar(i), passes_for_scalar(i), "s")
 
         def transpose_and_copy(i):
             raw_words = raw_of[i][:].bitcast(F32)
+            first_sorted = PASSES - passes_to_sort(i)
             grouped_of[i] = grouped_pool.tile([P, PASSES * BLOCK * 4], BF16, align_bytes=64, name="grouped", tag="grouped")
             grouped_words = grouped_of[i][:].bitcast(F32)
             for g in range(PASSES):
                 flipped = flip_psum.tile([P, 2, BLOCK], F32, tag="flip")
                 for u in range(2):
                     for s in range(ROWS_EACH):
-                        if (i, g) in sorted_of:
-                            tile, place = sorted_of[i, g]
-                            words = tile[:, s, place, u, :]
-                        else:
+                        if g < first_sorted:
                             words = raw_words[:, s, PASS_WORDS * g + u : PASS_WORDS * (g + 1) : 2]
+                        else:
+                            words = sorted_of[i][:, s, g - first_sorted, u, :]
                         nc.tensor.transpose(flipped[:, u, s * P : (s + 1) * P], words, ident_f32[:])
-                if g == 2 and i + 1 < UNITS:
-                    sort_on_scalar(i + 1)
                 to_vector = i >= 3 and (PASSES * i + g) % VECTOR_SHARE == 1
                 copy_out = nc.vector.tensor_copy if to_vector else nc.scalar.copy
                 copy_out(
@@ -322,45 +315,49 @@ def tile_layernormlstmcell_pb_kernel(
         step_at = {}
         for k, step in enumerate(STEPS):
             step_at[first_step_unit + k * (UNITS - first_step_unit) // len(STEPS)] = step
-        bias_behind = {9: ("o", 0), 10: ("o", 1)}
 
-        sort_on_vector(0)
+        sort_words(0)
         for i in range(UNITS + LAG):
             if i + PREFETCH == UNITS_PER_GATE:
                 nc.sync.dma_start(out=c_old[:], in_=c)
                 nc.sync.dma_start(out=ic_in[:], in_=ic_tilde)
             if i + PREFETCH < UNITS:
                 load(i + PREFETCH)
+            if i == PREFETCH:
+                for r in range(BIASES, len(vector_names)):
+                    load_vector(r)
             if i in step_at:
                 forget_step_on_vector(*step_at[i])
             if i + 1 < UNITS:
-                sort_on_vector(i + 1)
+                sort_words(i + 1)
             if i == 0:
                 quantise_activation("x")
+            if i == 2:
                 quantise_activation("h")
             if 1 <= i <= UNITS:
-                quantise(i - 1, parts=2 if i == UNITS else 1)
+                quantise(i - 1, parts=PASSES if i == UNITS else 1)
             if i < UNITS:
                 transpose_and_copy(i)
+            if i == 1:
+                flip_activation("h")
+            if i < 2:
+                spread_half("o_bias", i)
+                keep_bias("o", i)
             if i - 1 in step_at:
                 forget_step_on_scalar(*step_at[i - 1])
-            if i >= UNITS:
-                for half in range(2):
-                    spread_half("o_gain" if i == UNITS else "o_shift", half)
             if i >= LAG:
                 multiply(i - LAG)
                 bank_number, place = divmod(i - LAG, UNITS_PER_BANK)
                 if bank_number < 2 * CHUNKS - 1:
                     if place == UNITS_PER_BANK - 1:
                         add_bias_and_count(bank_number, 0, 2)
-                elif place % 2 == 1:
-                    add_bias_and_count(bank_number, place // 2, 1)
+                elif place >= 2:
+                    add_bias_and_count(bank_number, place - 2, 1)
                 if i - LAG == UNITS_PER_GATE - 1:
                     mean_and_rstd("f")
-            if i in bias_behind:
-                a, half = bias_behind[i]
-                spread_half(a + "_bias", half)
-                keep_bias(a, half)
+            if i >= UNITS:
+                for half in range(2):
+                    spread_half("o_gain" if i == UNITS else "o_shift", half)
             if i + 1 in step_at and step_at[i + 1][0] in ("gain", "shift"):
                 kind, half = step_at[i + 1]
                 spread_half("f_" + kind, half)
@@ -368,14 +365,13 @@ def tile_layernormlstmcell_pb_kernel(
         nc.sync.dma_start(out=out_1, in_=c_new[:])
 
         mean_and_rstd("o")
-        for chunks in ((0, 1), (2, 3)):
-            for chunk in chunks:
-                centre_and_gain("o", chunk_columns(chunk))
-            for chunk in chunks:
-                scale_and_shift("o", chunk_columns(chunk))
-                squash("o", chunk_columns(chunk))
-            multiplier = nc.gpsimd if 0 in chunks else nc.vector
-            for chunk in chunks:
-                cols = chunk_columns(chunk)
+        rest = (slice(2 * BANK, 3 * BANK), slice(3 * BANK, 3 * BANK + BLOCK), slice(3 * BANK + BLOCK, 4 * BANK))
+        for chunks, multiplier in (((chunk_columns(0), chunk_columns(1)), nc.gpsimd), (rest, nc.vector)):
+            for cols in chunks:
+                centre_and_gain("o", cols)
+            for cols in chunks:
+                scale_and_shift("o", cols)
+                squash("o", cols)
+            for cols in chunks:
                 multiplier.tensor_tensor(out=h_new[:, cols], in0=gate["o"][:, cols], in1=tanh_c[:, cols], op=ALU.mult)
                 nc.sync.dma_start(out=out_0[:, cols], in_=h_new[:, cols])

@@ -43,7 +43,7 @@ def tile_layernormlstmcell_pb_kernel(
         ctx.enter_context(tc.manual_schedule())
         keep = ctx.enter_context(tc.tile_pool(name="keep", bufs=1))
         stage = ctx.enter_context(tc.tile_pool(name="stage", bufs=2))
-        raw_pool = ctx.enter_context(tc.tile_pool(name="raw", bufs=6))
+        raw_pool = ctx.enter_context(tc.tile_pool(name="raw", bufs=8))
         sorted_pool = ctx.enter_context(tc.tile_pool(name="sorted", bufs=3))
         grouped_pool = ctx.enter_context(tc.tile_pool(name="grouped", bufs=3))
         packed_pool = ctx.enter_context(tc.tile_pool(name="packed", bufs=LAG + 2))
@@ -102,7 +102,10 @@ def tile_layernormlstmcell_pb_kernel(
             block, which = divmod(i % UNITS_PER_GATE, 2)
             rows = weights[a][which][block * BLOCK : (block + 1) * BLOCK, :]
             raw_of[i] = raw_pool.tile([P, ROWS_EACH, WIDTH], BF16, name="raw", tag="raw")
-            nc.sync.dma_start(out=raw_of[i][:], in_=rows.rearrange("(j s) k -> j s k", s=ROWS_EACH))
+            parts = 2 if i == UNITS - 1 else 1
+            for part in range(parts):
+                k = slice(part * WIDTH // parts, (part + 1) * WIDTH // parts)
+                nc.sync.dma_start(out=raw_of[i][:, :, k], in_=rows.rearrange("(j s) k -> j s k", s=ROWS_EACH)[:, :, k])
 
         act_raw = {}
 
@@ -206,7 +209,7 @@ def tile_layernormlstmcell_pb_kernel(
         def passes_to_sort(i):
             if i >= UNITS - 3 or i == 2:
                 return 0
-            return 2 if i < UNITS_PER_GATE else 1
+            return 2 if i < UNITS_PER_GATE or i % 2 == 1 else 1
 
         def sort_words(i):
             passes = passes_to_sort(i)
@@ -291,38 +294,42 @@ def tile_layernormlstmcell_pb_kernel(
             nc.vector.tensor_scalar_add(out=var_eps[a][:], in0=mean_var[a][:, 1:2], scalar1=EPS)
             nc.gpsimd.tensor_tensor(out=rstd[a][:], in0=var_eps[a][:], in1=minus_half[:], op=ALU.pow)
 
-        STEPS = ("gain", 0), ("gain", 1), ("shift", 0), ("shift", 1), ("mul", 0), ("mul", 1), ("add", 0), ("add", 1)
+        STEPS = ("gain", 0), ("gain", 1), ("shift", 0), ("shift", 1)
+        STEP_EVERY = 2
 
         def forget_step_on_vector(kind, half):
-            cols = half_columns(half)
             if kind == "gain":
-                centre_and_gain("f", cols)
-            elif kind == "shift":
-                scale_and_shift("f", cols)
-            elif kind == "mul":
-                nc.vector.tensor_mul(out=c_new[:, cols], in0=gate["f"][:, cols], in1=c_old[:, cols])
+                centre_and_gain("f", half_columns(half))
             else:
-                nc.vector.tensor_add(out=c_new[:, cols], in0=c_new[:, cols], in1=ic_in[:, cols])
-
-        def forget_step_on_scalar(kind, half):
-            cols = half_columns(half)
-            if kind == "shift":
-                squash("f", cols)
-            elif kind == "add":
-                nc.scalar.activation(out=tanh_c[:, cols], in_=c_new[:, cols], func=ACT.Tanh)
+                scale_and_shift("f", half_columns(half))
 
         first_step_unit = UNITS_PER_GATE + LAG + 1
-        step_at = {}
-        for k, step in enumerate(STEPS):
-            step_at[first_step_unit + k * (UNITS - first_step_unit) // len(STEPS)] = step
+        step_at = {first_step_unit + STEP_EVERY * k: step for k, step in enumerate(STEPS)}
+
+        def multiply_and_count(j):
+            multiply(j)
+            bank_number, place = divmod(j, UNITS_PER_BANK)
+            if bank_number < 2 * CHUNKS - 1:
+                if place == UNITS_PER_BANK - 1:
+                    add_bias_and_count(bank_number, 0, 2)
+            elif place % 2 == 1:
+                add_bias_and_count(bank_number, place // 2, 1)
+            if j == UNITS_PER_GATE - 1:
+                mean_and_rstd("f")
+
+        def forget_old_state(engine, cols):
+            engine.tensor_tensor(out=c_new[:, cols], in0=gate["f"][:, cols], in1=c_old[:, cols], op=ALU.mult)
+
+        def add_candidate(engine, cols):
+            engine.tensor_tensor(out=c_new[:, cols], in0=c_new[:, cols], in1=ic_in[:, cols], op=ALU.add)
 
         sort_words(0)
         for i in range(UNITS + LAG):
-            if i + PREFETCH == UNITS_PER_GATE:
-                nc.sync.dma_start(out=c_old[:], in_=c)
-                nc.sync.dma_start(out=ic_in[:], in_=ic_tilde)
             if i + PREFETCH < UNITS:
                 load(i + PREFETCH)
+            if i + PREFETCH == UNITS - 1:
+                nc.sync.dma_start(out=c_old[:], in_=c)
+                nc.sync.dma_start(out=ic_in[:], in_=ic_tilde)
             if i == PREFETCH:
                 for r in range(BIASES, len(vector_names)):
                     load_vector(r)
@@ -336,6 +343,8 @@ def tile_layernormlstmcell_pb_kernel(
                 quantise_activation("h")
             if 1 <= i <= UNITS:
                 quantise(i - 1, parts=PASSES if i == UNITS else 1)
+            if i == UNITS - 1:
+                multiply_and_count(i - LAG)
             if i < UNITS:
                 transpose_and_copy(i)
             if i == 1:
@@ -343,35 +352,49 @@ def tile_layernormlstmcell_pb_kernel(
             if i < 2:
                 spread_half("o_bias", i)
                 keep_bias("o", i)
-            if i - 1 in step_at:
-                forget_step_on_scalar(*step_at[i - 1])
-            if i >= LAG:
-                multiply(i - LAG)
-                bank_number, place = divmod(i - LAG, UNITS_PER_BANK)
-                if bank_number < 2 * CHUNKS - 1:
-                    if place == UNITS_PER_BANK - 1:
-                        add_bias_and_count(bank_number, 0, 2)
-                elif place >= 2:
-                    add_bias_and_count(bank_number, place - 2, 1)
-                if i - LAG == UNITS_PER_GATE - 1:
-                    mean_and_rstd("f")
-            if i >= UNITS:
-                for half in range(2):
-                    spread_half("o_gain" if i == UNITS else "o_shift", half)
-            if i + 1 in step_at and step_at[i + 1][0] in ("gain", "shift"):
+            if i - 1 in step_at and step_at[i - 1][0] == "shift":
+                squash("f", half_columns(step_at[i - 1][1]))
+            if i == UNITS:
+                forget_old_state(nc.vector, chunk_columns(0))
+            if i >= LAG and i != UNITS - 1:
+                multiply_and_count(i - LAG)
+            if i == UNITS:
+                spread_half("o_gain", 0)
+            if i + 1 in step_at:
                 kind, half = step_at[i + 1]
                 spread_half("f_" + kind, half)
+        spread_half("o_gain", 1)
+        for half in range(2):
+            spread_half("o_shift", half)
 
-        nc.sync.dma_start(out=out_1, in_=c_new[:])
-
+        for block in range(BANK // BLOCK, 3 * BANK // BLOCK):
+            forget_old_state(nc.gpsimd, slice(block * BLOCK, (block + 1) * BLOCK))
+        for chunk in (1, 2):
+            add_candidate(nc.gpsimd, chunk_columns(chunk))
+        forget_old_state(nc.gpsimd, chunk_columns(3))
         mean_and_rstd("o")
-        rest = (slice(2 * BANK, 3 * BANK), slice(3 * BANK, 3 * BANK + BLOCK), slice(3 * BANK + BLOCK, 4 * BANK))
-        for chunks, multiplier in (((chunk_columns(0), chunk_columns(1)), nc.gpsimd), (rest, nc.vector)):
-            for cols in chunks:
-                centre_and_gain("o", cols)
-            for cols in chunks:
-                scale_and_shift("o", cols)
-                squash("o", cols)
-            for cols in chunks:
-                multiplier.tensor_tensor(out=h_new[:, cols], in0=gate["o"][:, cols], in1=tanh_c[:, cols], op=ALU.mult)
-                nc.sync.dma_start(out=out_0[:, cols], in_=h_new[:, cols])
+        for chunk in (0, 3):
+            add_candidate(nc.gpsimd, chunk_columns(chunk))
+        for chunk in (1, 2, 0, 3):
+            nc.sync.dma_start(out=out_1[:, chunk_columns(chunk)], in_=c_new[:, chunk_columns(chunk)])
+
+        def tanh_of_state(chunk):
+            cols = chunk_columns(chunk)
+            nc.scalar.activation(out=tanh_c[:, cols], in_=c_new[:, cols], func=ACT.Tanh)
+
+        tanh_of_state(1)
+        tanh_of_state(2)
+        tanh_behind = {0: 0, 1: 3}
+        for chunks in ((0, 1), (2, 3)):
+            for chunk in chunks:
+                centre_and_gain("o", chunk_columns(chunk))
+            for chunk in chunks:
+                scale_and_shift("o", chunk_columns(chunk))
+                squash("o", chunk_columns(chunk))
+                if chunk in tanh_behind:
+                    tanh_of_state(tanh_behind[chunk])
+        for chunk in range(CHUNKS):
+            cols = chunk_columns(chunk)
+            multiplier = nc.gpsimd if chunk == 0 else nc.vector
+            multiplier.tensor_tensor(out=h_new[:, cols], in0=gate["o"][:, cols], in1=tanh_c[:, cols], op=ALU.mult)
+            nc.sync.dma_start(out=out_0[:, cols], in_=h_new[:, cols])

@@ -29,7 +29,6 @@ EPS = 1e-5
 LAG = 2
 PREFETCH = 3
 BIASES = 2
-VECTOR_SHARE = 32
 PASS_WORDS = K_PASS // 2
 
 FLOPS = 2 * P * (2 * WIDTH) * (2 * WIDTH)
@@ -53,14 +52,12 @@ def tile_layernormlstmcell_pb_kernel(
         ident_f32 = keep.tile([P, P], F32)
         make_identity(nc, ident_f32[:])
         ident_bf16 = keep.tile([P, P], BF16)
-        make_identity(nc, ident_bf16[:])
         minus_half = keep.tile([P, 1], F32)
         nc.vector.memset(minus_half[:], -0.5)
 
         vectors = {"f_bias": Wf_b, "o_bias": Wo_b, "f_gain": lnf_g, "f_shift": lnf_b, "o_gain": lno_g, "o_shift": lno_b}
         vector_names = list(vectors)
         vector_rows = keep.tile([P, WIDTH], BF16)
-        nc.vector.memset(vector_rows[:].bitcast(I32), 0)
         bias_rows = keep.tile([P, WIDTH], BF16)
         nc.vector.memset(bias_rows[:].bitcast(I32), 0)
 
@@ -70,6 +67,7 @@ def tile_layernormlstmcell_pb_kernel(
 
         table_warm = keep.tile([P, 1], F32)
         nc.scalar.activation(out=table_warm[:], in_=minus_half[:], func=ACT.Sigmoid)
+        nc.scalar.copy(out=ident_bf16[:], in_=ident_f32[:])
 
         in_psum = {}
 
@@ -114,9 +112,9 @@ def tile_layernormlstmcell_pb_kernel(
             nc.sync.dma_start(out=act_raw[name][:], in_=source)
 
         load_activation("x", x)
+        load(0)
         for r in range(BIASES):
             load_vector(r)
-        load(0)
         load(1)
         load_activation("h", h)
         for i in range(2, PREFETCH):
@@ -145,9 +143,6 @@ def tile_layernormlstmcell_pb_kernel(
             act_scales[name] = keep.tile([P, PASSES * P], U8, align_bytes=64, name="scales_" + name)
             act_grouped_of[name] = act_grouped
         flip_activation("x")
-        for half in range(2):
-            spread_half("f_bias", half)
-            keep_bias("f", half)
 
         def quantise_activation(name):
             nc.vector.quantize_mx(
@@ -237,9 +232,7 @@ def tile_layernormlstmcell_pb_kernel(
                         else:
                             words = sorted_of[i][:, s, g - first_sorted, u, :]
                         nc.tensor.transpose(flipped[:, u, s * P : (s + 1) * P], words, ident_f32[:])
-                to_vector = i >= 3 and (PASSES * i + g) % VECTOR_SHARE == 1
-                copy_out = nc.vector.tensor_copy if to_vector else nc.scalar.copy
-                copy_out(
+                nc.scalar.copy(
                     out=grouped_words[:, g * BANK : (g + 1) * BANK].rearrange("p (n u) -> p n u", u=2),
                     in_=flipped[:].rearrange("p u n -> p n u"),
                 )
@@ -294,14 +287,17 @@ def tile_layernormlstmcell_pb_kernel(
             nc.vector.tensor_scalar_add(out=var_eps[a][:], in0=mean_var[a][:, 1:2], scalar1=EPS)
             nc.gpsimd.tensor_tensor(out=rstd[a][:], in0=var_eps[a][:], in1=minus_half[:], op=ALU.pow)
 
-        STEPS = ("gain", 0), ("gain", 1), ("shift", 0), ("shift", 1)
+        STEPS = ("gain", 0), ("gain", 1), ("shift", 0), ("shift", 1), ("forget", 0), ("forget", 1)
         STEP_EVERY = 2
 
         def forget_step_on_vector(kind, half):
+            cols = half_columns(half)
             if kind == "gain":
-                centre_and_gain("f", half_columns(half))
+                centre_and_gain("f", cols)
+            elif kind == "shift":
+                scale_and_shift("f", cols)
             else:
-                scale_and_shift("f", half_columns(half))
+                nc.vector.tensor_mul(out=c_new[:, cols], in0=gate["f"][:, cols], in1=c_old[:, cols])
 
         first_step_unit = UNITS_PER_GATE + LAG + 1
         step_at = {first_step_unit + STEP_EVERY * k: step for k, step in enumerate(STEPS)}
@@ -317,18 +313,18 @@ def tile_layernormlstmcell_pb_kernel(
             if j == UNITS_PER_GATE - 1:
                 mean_and_rstd("f")
 
-        def forget_old_state(engine, cols):
-            engine.tensor_tensor(out=c_new[:, cols], in0=gate["f"][:, cols], in1=c_old[:, cols], op=ALU.mult)
-
-        def add_candidate(engine, cols):
+        def add_candidate(engine, chunk):
+            cols = chunk_columns(chunk)
             engine.tensor_tensor(out=c_new[:, cols], in0=c_new[:, cols], in1=ic_in[:, cols], op=ALU.add)
 
         sort_words(0)
+        nc.vector.memset(vector_rows[:].bitcast(I32), 0)
         for i in range(UNITS + LAG):
             if i + PREFETCH < UNITS:
                 load(i + PREFETCH)
-            if i + PREFETCH == UNITS - 1:
+            if i + PREFETCH == UNITS_PER_GATE:
                 nc.sync.dma_start(out=c_old[:], in_=c)
+            if i + PREFETCH == UNITS - 1:
                 nc.sync.dma_start(out=ic_in[:], in_=ic_tilde)
             if i == PREFETCH:
                 for r in range(BIASES, len(vector_names)):
@@ -349,52 +345,44 @@ def tile_layernormlstmcell_pb_kernel(
                 transpose_and_copy(i)
             if i == 1:
                 flip_activation("h")
-            if i < 2:
-                spread_half("o_bias", i)
-                keep_bias("o", i)
+            if i < 4:
+                spread_half(vector_names[i // 2], i % 2)
+                keep_bias(vector_names[i // 2][0], i % 2)
             if i - 1 in step_at and step_at[i - 1][0] == "shift":
                 squash("f", half_columns(step_at[i - 1][1]))
             if i == UNITS:
-                forget_old_state(nc.vector, chunk_columns(0))
+                add_candidate(nc.vector, 0)
             if i >= LAG and i != UNITS - 1:
                 multiply_and_count(i - LAG)
             if i == UNITS:
                 spread_half("o_gain", 0)
-            if i + 1 in step_at:
+            if i + 1 in step_at and step_at[i + 1][0] != "forget":
                 kind, half = step_at[i + 1]
                 spread_half("f_" + kind, half)
         spread_half("o_gain", 1)
         for half in range(2):
             spread_half("o_shift", half)
 
-        for block in range(BANK // BLOCK, 3 * BANK // BLOCK):
-            forget_old_state(nc.gpsimd, slice(block * BLOCK, (block + 1) * BLOCK))
-        for chunk in (1, 2):
-            add_candidate(nc.gpsimd, chunk_columns(chunk))
-        forget_old_state(nc.gpsimd, chunk_columns(3))
         mean_and_rstd("o")
-        for chunk in (0, 3):
-            add_candidate(nc.gpsimd, chunk_columns(chunk))
-        for chunk in (1, 2, 0, 3):
+        for chunk in range(1, CHUNKS):
+            add_candidate(nc.gpsimd, chunk)
+        for chunk in range(CHUNKS):
             nc.sync.dma_start(out=out_1[:, chunk_columns(chunk)], in_=c_new[:, chunk_columns(chunk)])
 
         def tanh_of_state(chunk):
             cols = chunk_columns(chunk)
             nc.scalar.activation(out=tanh_c[:, cols], in_=c_new[:, cols], func=ACT.Tanh)
 
-        tanh_of_state(1)
-        tanh_of_state(2)
-        tanh_behind = {0: 0, 1: 3}
+        tanh_of_state(0)
         for chunks in ((0, 1), (2, 3)):
             for chunk in chunks:
                 centre_and_gain("o", chunk_columns(chunk))
             for chunk in chunks:
                 scale_and_shift("o", chunk_columns(chunk))
                 squash("o", chunk_columns(chunk))
-                if chunk in tanh_behind:
-                    tanh_of_state(tanh_behind[chunk])
+                if chunk + 1 < CHUNKS:
+                    tanh_of_state(chunk + 1)
         for chunk in range(CHUNKS):
             cols = chunk_columns(chunk)
-            multiplier = nc.gpsimd if chunk == 0 else nc.vector
-            multiplier.tensor_tensor(out=h_new[:, cols], in0=gate["o"][:, cols], in1=tanh_c[:, cols], op=ALU.mult)
+            nc.vector.tensor_mul(out=h_new[:, cols], in0=gate["o"][:, cols], in1=tanh_c[:, cols])
             nc.sync.dma_start(out=out_0[:, cols], in_=h_new[:, cols])

from contextlib import ExitStack

import concourse.mybir as mybir
from concourse.masks import make_identity

F32 = mybir.dt.float32
BF16 = mybir.dt.bfloat16
U32 = mybir.dt.uint32
U8 = mybir.dt.uint8
I32 = mybir.dt.int32
FP8X4 = mybir.dt.float8_e4m3fn_x4
ALU = mybir.AluOpType
ACT = mybir.ActivationFunctionType

P = 128
WIDTH = 2048
K_PASS = 512
PASSES = WIDTH // K_PASS
BLOCK = 256
ROWS_EACH = BLOCK // P
BANK = 512
CHUNKS = WIDTH // BANK
HALF = WIDTH // 2
UNITS_PER_GATE = 2 * WIDTH // BLOCK
UNITS = 2 * UNITS_PER_GATE
UNITS_PER_BANK = 2 * BANK // BLOCK
EPS = 1e-5

LAG = 2
PREFETCH = 3
BIASES = 2
PASS_WORDS = K_PASS // 2

FLOPS = 2 * P * (2 * WIDTH) * (2 * WIDTH)


def tile_layernormlstmcell_pb_kernel(
    tc, x, h, c, ic_tilde, Wf_w, Wf_b, Uf_w, lnf_g, lnf_b, Wo_w, Wo_b, Uo_w, lno_g, lno_b, out_0, out_1
):
    nc = tc.nc
    with ExitStack() as ctx:
        ctx.enter_context(tc.manual_schedule())
        keep = ctx.enter_context(tc.tile_pool(name="keep", bufs=1))
        stage = ctx.enter_context(tc.tile_pool(name="stage", bufs=2))
        raw_pool = ctx.enter_context(tc.tile_pool(name="raw", bufs=8))
        sorted_pool = ctx.enter_context(tc.tile_pool(name="sorted", bufs=3))
        grouped_pool = ctx.enter_context(tc.tile_pool(name="grouped", bufs=3))
        packed_pool = ctx.enter_context(tc.tile_pool(name="packed", bufs=LAG + 2))
        flip_psum = ctx.enter_context(tc.psum_pool(name="flip", bufs=6))
        sum_psum = ctx.enter_context(tc.psum_pool(name="sums", bufs=2))

        ident_f32 = keep.tile([P, P], F32)
        make_identity(nc, ident_f32[:])
        ident_bf16 = keep.tile([P, P], BF16)
        minus_half = keep.tile([P, 1], F32)
        nc.vector.memset(minus_half[:], -0.5)

        vectors = {"f_bias": Wf_b, "o_bias": Wo_b, "f_gain": lnf_g, "f_shift": lnf_b, "o_gain": lno_g, "o_shift": lno_b}
        vector_names = list(vectors)
        vector_rows = keep.tile([P, WIDTH], BF16)
        bias_rows = keep.tile([P, WIDTH], BF16)
        nc.vector.memset(bias_rows[:].bitcast(I32), 0)

        def load_vector(r):
            rows = bias_rows if r < BIASES else vector_rows
            nc.sync.dma_start(out=rows[r : r + 1, :], in_=vectors[vector_names[r]].rearrange("(o n) -> o n", o=1))

        table_warm = keep.tile([P, 1], F32)
        nc.scalar.activation(out=table_warm[:], in_=minus_half[:], func=ACT.Sigmoid)
        nc.scalar.copy(out=ident_bf16[:], in_=ident_f32[:])

        in_psum = {}

        def spread_half(name, half):
            r = vector_names.index(name)
            rows = bias_rows if r < BIASES else vector_rows
            in_psum[name, half] = flip_psum.tile([P, HALF], BF16, name="flip", tag="flip")
            for q in range(HALF // BANK):
                first = half * HALF + q * BANK
                nc.tensor.matmul(
                    out=in_psum[name, half][:, q * BANK : (q + 1) * BANK],
                    lhsT=ident_bf16[:, r : r + 1].to_broadcast([P, P]),
                    rhs=rows[:, first : first + BANK],
                    start=True,
                    stop=True,
                )

        bias = {}
        for a in ("f", "o"):
            bias[a] = keep.tile([P, WIDTH], BF16, name="bias_" + a)

        def keep_bias(a, half):
            nc.scalar.copy(out=bias[a][:, half * HALF : (half + 1) * HALF], in_=in_psum[a + "_bias", half][:])

        weights = {"f": (Wf_w, Uf_w), "o": (Wo_w, Uo_w)}
        raw_of = {}

        def load(i):
            a = "f" if i < UNITS_PER_GATE else "o"
            block, which = divmod(i % UNITS_PER_GATE, 2)
            rows = weights[a][which][block * BLOCK : (block + 1) * BLOCK, :]
            raw_of[i] = raw_pool.tile([P, ROWS_EACH, WIDTH], BF16, name="raw", tag="raw")
            parts = 2 if i == UNITS - 1 else 1
            for part in range(parts):
                k = slice(part * WIDTH // parts, (part + 1) * WIDTH // parts)
                nc.sync.dma_start(out=raw_of[i][:, :, k], in_=rows.rearrange("(j s) k -> j s k", s=ROWS_EACH)[:, :, k])

        act_raw = {}

        def load_activation(name, source):
            act_raw[name] = keep.tile([P, WIDTH], BF16, name="raw_" + name)
            nc.sync.dma_start(out=act_raw[name][:], in_=source)

        load_activation("x", x)
        load(0)
        for r in range(BIASES):
            load_vector(r)
        load(1)
        load_activation("h", h)
        for i in range(2, PREFETCH):
            load(i)

        act_codes = {}
        act_scales = {}
        act_grouped_of = {}

        def flip_activation(name):
            act_words = act_raw[name][:].bitcast(F32)
            act_grouped = stage.tile([P, PASSES * P * 4], BF16, align_bytes=64)
            act_grouped_words = act_grouped[:].bitcast(F32)
            for pair in range(PASSES // 2):
                flipped = flip_psum.tile([P, 2, 2, P], F32, tag="flip")
                for g in (2 * pair, 2 * pair + 1):
                    for u in range(2):
                        words = slice(2 * P * g + u, 2 * P * (g + 1), 2)
                        nc.tensor.transpose(flipped[:, g % 2, u, :], act_words[:, words], ident_f32[:])
                copy_out = nc.scalar.copy if pair == 0 else nc.vector.tensor_copy
                copy_out(
                    out=act_grouped_words[:, pair * BANK : (pair + 1) * BANK].rearrange("p (g b u) -> p g b u", g=2, u=2),
                    in_=flipped[:].rearrange("p g u b -> p g b u"),
                )
            act_codes[name] = keep.tile([P, PASSES * P], U32, align_bytes=64, name="codes_" + name)
            act_scales[name] = keep.tile([P, PASSES * P], U8, align_bytes=64, name="scales_" + name)
            act_grouped_of[name] = act_grouped
        flip_activation("x")

        def quantise_activation(name):
            nc.vector.quantize_mx(
                out=act_codes[name][:].bitcast(FP8X4), scales=act_scales[name][:], in_=act_grouped_of[name][:]
            )


        pre = {}
        gate = {}
        stats = {}
        stats_slots = {"f": 0, "o": 0}
        mean_var = {}
        var_eps = {}
        rstd = {}
        for a in ("f", "o"):
            pre[a] = keep.tile([P, WIDTH], F32, name="pre_" + a)
            gate[a] = keep.tile([P, WIDTH], F32, name="gate_" + a)
            stats[a] = keep.tile([P, CHUNKS + 1, 6], F32, name="stats_" + a)
            mean_var[a] = keep.tile([P, 2], F32, name="mean_var_" + a)
            var_eps[a] = keep.tile([P, 1], F32, name="var_eps_" + a)
            rstd[a] = keep.tile([P, 1], F32, name="rstd_" + a)
        c_old = keep.tile([P, WIDTH], BF16)
        ic_in = keep.tile([P, WIDTH], BF16)
        c_new = keep.tile([P, WIDTH], F32)
        tanh_c = keep.tile([P, WIDTH], F32)
        h_new = keep.tile([P, WIDTH], F32)

        def chunk_columns(chunk):
            return slice(chunk * BANK, (chunk + 1) * BANK)

        def half_columns(half):
            return slice(half * HALF, (half + 1) * HALF)

        def spread_columns(name, cols):
            first = cols.start % HALF
            return in_psum[name, cols.start // HALF][:, first : first + cols.stop - cols.start]

        def centre_and_gain(a, cols):
            nc.vector.scalar_tensor_tensor(
                out=pre[a][:, cols], in0=pre[a][:, cols], scalar=mean_var[a][:, 0:1],
                in1=spread_columns(a + "_gain", cols), op0=ALU.subtract, op1=ALU.mult,
            )

        def scale_and_shift(a, cols):
            nc.vector.scalar_tensor_tensor(
                out=pre[a][:, cols], in0=pre[a][:, cols], scalar=rstd[a][:, 0:1],
                in1=spread_columns(a + "_shift", cols), op0=ALU.mult, op1=ALU.add,
            )

        def squash(a, cols):
            nc.scalar.activation(out=gate[a][:, cols], in_=pre[a][:, cols], func=ACT.Sigmoid)

        sorted_of = {}
        grouped_of = {}
        codes_of = {}
        scales_of = {}
        sums_of = {}

        def passes_to_sort(i):
            if i >= UNITS - 3 or i == 2:
                return 0
            return 2 if i < UNITS_PER_GATE or i % 2 == 1 else 1

        def sort_words(i):
            passes = passes_to_sort(i)
            if passes == 0:
                return
            sorted_of[i] = sorted_pool.tile([P, ROWS_EACH, passes, 2, P], F32, name="sorted", tag="sorted")
            nc.vector.tensor_copy(
                out=sorted_of[i][:],
                in_=raw_of[i][:].bitcast(F32)[:, :, (PASSES - passes) * PASS_WORDS :].rearrange(
                    "p s (g x u) -> p s g u x", g=passes, u=2
                ),
            )

        def transpose_and_copy(i):
            raw_words = raw_of[i][:].bitcast(F32)
            first_sorted = PASSES - passes_to_sort(i)
            grouped_of[i] = grouped_pool.tile([P, PASSES * BLOCK * 4], BF16, align_bytes=64, name="grouped", tag="grouped")
            grouped_words = grouped_of[i][:].bitcast(F32)
            for g in range(PASSES):
                flipped = flip_psum.tile([P, 2, BLOCK], F32, tag="flip")
                for u in range(2):
                    for s in range(ROWS_EACH):
                        if g < first_sorted:
                            words = raw_words[:, s, PASS_WORDS * g + u : PASS_WORDS * (g + 1) : 2]
                        else:
                            words = sorted_of[i][:, s, g - first_sorted, u, :]
                        nc.tensor.transpose(flipped[:, u, s * P : (s + 1) * P], words, ident_f32[:])
                nc.scalar.copy(
                    out=grouped_words[:, g * BANK : (g + 1) * BANK].rearrange("p (n u) -> p n u", u=2),
                    in_=flipped[:].rearrange("p u n -> p n u"),
                )

        def quantise(i, parts=1):
            codes_of[i] = packed_pool.tile([P, PASSES * BLOCK], U32, align_bytes=64, name="codes", tag="codes")
            scales_of[i] = packed_pool.tile([P, PASSES * BLOCK], U8, align_bytes=64, name="scales", tag="scales")
            width = PASSES * BLOCK // parts
            for part in range(parts):
                cols = slice(part * width, (part + 1) * width)
                nc.vector.quantize_mx(
                    out=codes_of[i][:, cols].bitcast(FP8X4),
                    scales=scales_of[i][:, cols],
                    in_=grouped_of[i][:, 4 * cols.start : 4 * cols.stop],
                )

        def multiply(i):
            bank_number, place = divmod(i, UNITS_PER_BANK)
            block_in_bank, which = divmod(place, 2)
            if place == 0:
                sums_of[bank_number] = sum_psum.tile([P, BANK], F32, name="sums", tag="sums")
            name = "x" if which == 0 else "h"
            for g in range(PASSES):
                nc.tensor.matmul_mx(
                    out=sums_of[bank_number][:, block_in_bank * BLOCK : (block_in_bank + 1) * BLOCK],
                    lhsT=act_codes[name][:, g * P : (g + 1) * P].bitcast(FP8X4),
                    lhsT_scale=act_scales[name][:, g * P : (g + 1) * P],
                    rhs=codes_of[i][:, g * BLOCK : (g + 1) * BLOCK].bitcast(FP8X4),
                    rhs_scale=scales_of[i][:, g * BLOCK : (g + 1) * BLOCK],
                    start=(which == 0 and g == 0),
                    stop=(which == 1 and g == PASSES - 1),
                )

        def add_bias_and_count(bank_number, first_block, blocks):
            a = "f" if bank_number < CHUNKS else "o"
            chunk = bank_number % CHUNKS
            first = chunk * BANK + first_block * BLOCK
            cols = slice(first, first + blocks * BLOCK)
            sums = sums_of[bank_number][:, first_block * BLOCK : (first_block + blocks) * BLOCK]
            slot = stats_slots[a]
            stats_slots[a] += 1
            nc.vector.tensor_tensor(
                out=pre[a][:, cols].rearrange("p (b j s) -> p b j s", b=blocks, s=ROWS_EACH),
                in0=sums.rearrange("p (b s j) -> p b j s", b=blocks, s=ROWS_EACH),
                in1=bias[a][:, cols].rearrange("p (b j s) -> p b j s", b=blocks, s=ROWS_EACH),
                op=ALU.add,
            )
            nc.vector.bn_stats(out=stats[a][:, slot, :], in_=pre[a][:, cols])

        def mean_and_rstd(a):
            nc.vector.bn_aggr(out=mean_var[a][:], in_=stats[a][:, : stats_slots[a], :].rearrange("p n six -> p (n six)"))
            nc.vector.tensor_scalar_add(out=var_eps[a][:], in0=mean_var[a][:, 1:2], scalar1=EPS)
            nc.gpsimd.tensor_tensor(out=rstd[a][:], in0=var_eps[a][:], in1=minus_half[:], op=ALU.pow)

        STEPS = ("gain", 0), ("gain", 1), ("shift", 0), ("shift", 1), ("forget", 0), ("forget", 1)
        STEP_EVERY = 2

        def forget_step_on_vector(kind, half):
            cols = half_columns(half)
            if kind == "gain":
                centre_and_gain("f", cols)
            elif kind == "shift":
                scale_and_shift("f", cols)
            else:
                nc.vector.tensor_mul(out=c_new[:, cols], in0=gate["f"][:, cols], in1=c_old[:, cols])

        first_step_unit = UNITS_PER_GATE + LAG + 1
        step_at = {first_step_unit + STEP_EVERY * k: step for k, step in enumerate(STEPS)}

        def multiply_and_count(j):
            multiply(j)
            bank_number, place = divmod(j, UNITS_PER_BANK)
            if bank_number < 2 * CHUNKS - 1:
                if place == UNITS_PER_BANK - 1:
                    add_bias_and_count(bank_number, 0, 2)
            elif place % 2 == 1:
                add_bias_and_count(bank_number, place // 2, 1)
            if j == UNITS_PER_GATE - 1:
                mean_and_rstd("f")

        def add_candidate(engine, chunk):
            cols = chunk_columns(chunk)
            engine.tensor_tensor(out=c_new[:, cols], in0=c_new[:, cols], in1=ic_in[:, cols], op=ALU.add)

        sort_words(0)
        nc.vector.memset(vector_rows[:].bitcast(I32), 0)
        for i in range(UNITS + LAG):
            if i + PREFETCH < UNITS:
                load(i + PREFETCH)
            if i + PREFETCH == UNITS_PER_GATE:
                nc.sync.dma_start(out=c_old[:], in_=c)
            if i + PREFETCH == UNITS - 1:
                nc.sync.dma_start(out=ic_in[:], in_=ic_tilde)
            if i == PREFETCH:
                for r in range(BIASES, len(vector_names)):
                    load_vector(r)
            if i in step_at:
                forget_step_on_vector(*step_at[i])
            if i + 1 < UNITS:
                sort_words(i + 1)
            if i == 0:
                quantise_activation("x")
            if i == 2:
                quantise_activation("h")
            if 1 <= i <= UNITS:
                quantise(i - 1, parts=PASSES if i == UNITS else 1)
            if i == UNITS - 1:
                multiply_and_count(i - LAG)
            if i < UNITS:
                transpose_and_copy(i)
            if i == 1:
                flip_activation("h")
            if i < 4:
                spread_half(vector_names[i // 2], i % 2)
                keep_bias(vector_names[i // 2][0], i % 2)
            if i - 1 in step_at and step_at[i - 1][0] == "shift":
                squash("f", half_columns(step_at[i - 1][1]))
            if i == UNITS:
                add_candidate(nc.vector, 0)
            if i >= LAG and i != UNITS - 1:
                multiply_and_count(i - LAG)
            if i == UNITS:
                spread_half("o_gain", 0)
            if i + 1 in step_at and step_at[i + 1][0] != "forget":
                kind, half = step_at[i + 1]
                spread_half("f_" + kind, half)
        spread_half("o_gain", 1)
        for half in range(2):
            spread_half("o_shift", half)

        mean_and_rstd("o")
        for chunk in range(1, CHUNKS):
            add_candidate(nc.gpsimd, chunk)
        for chunk in range(CHUNKS):
            nc.sync.dma_start(out=out_1[:, chunk_columns(chunk)], in_=c_new[:, chunk_columns(chunk)])

        def tanh_of_state(chunk):
            cols = chunk_columns(chunk)
            nc.scalar.activation(out=tanh_c[:, cols], in_=c_new[:, cols], func=ACT.Tanh)

        tanh_of_state(0)
        for chunks in ((0, 1), (2, 3)):
            for chunk in chunks:
                centre_and_gain("o", chunk_columns(chunk))
            for chunk in chunks:
                scale_and_shift("o", chunk_columns(chunk))
                squash("o", chunk_columns(chunk))
                if chunk + 1 < CHUNKS:
                    tanh_of_state(chunk + 1)
        for chunk in range(CHUNKS):
            cols = chunk_columns(chunk)
            nc.vector.tensor_mul(out=h_new[:, cols], in0=gate["o"][:, cols], in1=tanh_c[:, cols])
            nc.sync.dma_start(out=out_0[:, cols], in_=h_new[:, cols])
